import numpy as np
import ml_dtypes

BF16 = ml_dtypes.bfloat16


def bf(x):
    return np.asarray(x, np.float32).astype(BF16)


def f32(x):
    return np.asarray(x, np.float32)


def f64(x):
    return np.asarray(x).astype(np.float64)


def striped(idx):
    return np.tile(idx.reshape(-1, 16).T, (8, 1))


C, S, N = 512, 256, 512


def embed_position(d):
    i = np.arange(d)
    ep = 1.0 / np.power(10000.0, (i - i % 2) / float(d))
    ang = i * ep
    return np.where(i % 2 == 1, np.cos(ang), np.sin(ang))


def setup_inputs():
    return {"table": f32(np.random.standard_normal((C, S))), "pos": f32(embed_position(C).reshape(C, 1)), "offs": striped(np.random.permutation(np.tile(np.arange(S), 2))[:N])}


def reference(table, pos, offs):
    idx = offs[:16].T.reshape(-1)
    return f64(table)[:, idx] + f64(pos)

@@ -1,0 +1,43 @@
+import concourse.mybir as mybir
+
+F32, U16 = mybir.dt.float32, mybir.dt.uint16
+ADD = mybir.AluOpType.add
+COPY = mybir.ActivationFunctionType.Copy
+P = 128
+
+
+def tile_inpembed_kernel(tc, table, pos, offs, out):
+    nc = tc.nc
+    features, words = table.shape
+    tokens = out.shape[1]
+    blocks = features // P
+    piece = words
+    pieces = tokens // piece
+
+    with tc.tile_pool(name="held", bufs=1) as held:
+        offsets = held.tile([P, tokens // 16], U16, name="offsets")
+        nc.sync.dma_start(offsets[:], offs)
+
+        pos_cols = held.tile([P, blocks], F32, name="pos_cols")
+        with nc.allow_non_contiguous_dma(reason="512 floats, one to a partition and block"):
+            nc.scalar.dma_start(pos_cols[:], pos.rearrange("(b p) o -> p (b o)", p=P))
+
+        windows = [held.tile([P, words], F32, name=f"window{b}") for b in range(blocks)]
+        for b in range(blocks):
+            queue = nc.sync if b % 2 == 0 else nc.scalar
+            queue.dma_start(windows[b][:], table[b * P : (b + 1) * P, :])
+
+        for b in range(blocks):
+            pos_wide = held.tile([P, piece], F32, name=f"pos_wide{b}")
+            nc.scalar.activation(pos_wide[:], pos_cols[:, b : b + 1].to_broadcast([P, piece]), COPY)
+
+            embedded = held.tile([P, tokens], F32, name=f"embedded{b}")
+            for k in range(pieces):
+                nc.vector.tensor_tensor(
+                    embedded[:, k * piece : (k + 1) * piece],
+                    windows[b][:].indirect(offsets[:, k * (piece // 16) : (k + 1) * (piece // 16)]),
+                    pos_wide[:],
+                    ADD,
+                )
+            queue = nc.sync if b % 2 == 0 else nc.scalar
+            queue.dma_start(out[b * P : (b + 1) * P, :], embedded[:])

@@ -39,5 +39,8 @@ def tile_inpembed_kernel(tc, table, pos, offs, out):
                     pos_wide[:],
                     ADD,
                 )
-            queue = nc.sync if b % 2 == 0 else nc.scalar
-            queue.dma_start(out[b * P : (b + 1) * P, :], embedded[:])
+                queue = nc.sync if k % 2 == 0 else nc.scalar
+                queue.dma_start(
+                    out[b * P : (b + 1) * P, k * piece : (k + 1) * piece],
+                    embedded[:, k * piece : (k + 1) * piece],
+                )

@@ -24,8 +24,7 @@ def tile_inpembed_kernel(tc, table, pos, offs, out):
 
         windows = [held.tile([P, words], F32, name=f"window{b}") for b in range(blocks)]
         for b in range(blocks):
-            queue = nc.sync if b % 2 == 0 else nc.scalar
-            queue.dma_start(windows[b][:], table[b * P : (b + 1) * P, :])
+            nc.sync.dma_start(windows[b][:], table[b * P : (b + 1) * P, :])
 
         for b in range(blocks):
             pos_wide = held.tile([P, piece], F32, name=f"pos_wide{b}")

@@ -14,17 +14,21 @@ def tile_inpembed_kernel(tc, table, pos, offs, out):
     piece = words
     pieces = tokens // piece
 
+    table_blocks = table.rearrange("(p b) s -> p b s", b=blocks)
+    pos_blocks = pos.rearrange("(p b) o -> p (b o)", b=blocks)
+    out_blocks = out.rearrange("(p b) n -> p b n", b=blocks)
+
     with tc.tile_pool(name="held", bufs=1) as held:
         offsets = held.tile([P, tokens // 16], U16, name="offsets")
         nc.sync.dma_start(offsets[:], offs)
 
         pos_cols = held.tile([P, blocks], F32, name="pos_cols")
-        with nc.allow_non_contiguous_dma(reason="512 floats, one to a partition and block"):
-            nc.scalar.dma_start(pos_cols[:], pos.rearrange("(b p) o -> p (b o)", p=P))
+        nc.scalar.dma_start(pos_cols[:], pos_blocks)
 
         windows = [held.tile([P, words], F32, name=f"window{b}") for b in range(blocks)]
         for b in range(blocks):
-            nc.sync.dma_start(windows[b][:], table[b * P : (b + 1) * P, :])
+            queue = nc.sync if b % 2 == 0 else nc.scalar
+            queue.dma_start(windows[b][:], table_blocks[:, b, :])
 
         for b in range(blocks):
             pos_wide = held.tile([P, piece], F32, name=f"pos_wide{b}")
@@ -40,6 +44,6 @@ def tile_inpembed_kernel(tc, table, pos, offs, out):
                 )
                 queue = nc.sync if k % 2 == 0 else nc.scalar
                 queue.dma_start(
-                    out[b * P : (b + 1) * P, k * piece : (k + 1) * piece],
+                    out_blocks[:, b, k * piece : (k + 1) * piece],
                     embedded[:, k * piece : (k + 1) * piece],
                 )

@@ -32,7 +32,11 @@ def tile_inpembed_kernel(tc, table, pos, offs, out):
 
         for b in range(blocks):
             pos_wide = held.tile([P, piece], F32, name=f"pos_wide{b}")
-            nc.scalar.activation(pos_wide[:], pos_cols[:, b : b + 1].to_broadcast([P, piece]), COPY)
+            pos_repeated = pos_cols[:, b : b + 1].to_broadcast([P, piece])
+            if b == 0:
+                nc.vector.tensor_copy(pos_wide[:], pos_repeated)
+            else:
+                nc.scalar.activation(pos_wide[:], pos_repeated, COPY)
 
             embedded = held.tile([P, tokens], F32, name=f"embedded{b}")
             for k in range(pieces):

@@ -38,16 +38,22 @@ def tile_inpembed_kernel(tc, table, pos, offs, out):
             else:
                 nc.scalar.activation(pos_wide[:], pos_repeated, COPY)
 
+            widths = [piece] * pieces
+            if b == blocks - 1:
+                widths[-1:] = [piece // 2, piece // 4, piece // 4]
+
             embedded = held.tile([P, tokens], F32, name=f"embedded{b}")
-            for k in range(pieces):
+            first = 0
+            for k, width in enumerate(widths):
                 nc.vector.tensor_tensor(
-                    embedded[:, k * piece : (k + 1) * piece],
-                    windows[b][:].indirect(offsets[:, k * (piece // 16) : (k + 1) * (piece // 16)]),
-                    pos_wide[:],
+                    embedded[:, first : first + width],
+                    windows[b][:].indirect(offsets[:, first // 16 : (first + width) // 16]),
+                    pos_wide[:, :width],
                     ADD,
                 )
                 queue = nc.sync if k % 2 == 0 else nc.scalar
                 queue.dma_start(
-                    out_blocks[:, b, k * piece : (k + 1) * piece],
-                    embedded[:, k * piece : (k + 1) * piece],
+                    out_blocks[:, b, first : first + width],
+                    embedded[:, first : first + width],
                 )
+                first += width

@@ -19,16 +19,15 @@ def tile_inpembed_kernel(tc, table, pos, offs, out):
     out_blocks = out.rearrange("(p b) n -> p b n", b=blocks)
 
     with tc.tile_pool(name="held", bufs=1) as held:
-        offsets = held.tile([P, tokens // 16], U16, name="offsets")
-        nc.sync.dma_start(offsets[:], offs)
-
         pos_cols = held.tile([P, blocks], F32, name="pos_cols")
-        nc.scalar.dma_start(pos_cols[:], pos_blocks)
-
+        offsets = held.tile([P, tokens // 16], U16, name="offsets")
         windows = [held.tile([P, words], F32, name=f"window{b}") for b in range(blocks)]
-        for b in range(blocks):
-            queue = nc.sync if b % 2 == 0 else nc.scalar
-            queue.dma_start(windows[b][:], table_blocks[:, b, :])
+        nc.sync.dma_start(pos_cols[:], pos_blocks)
+        nc.scalar.dma_start(windows[0][:], table_blocks[:, 0, :])
+        nc.sync.dma_start(offsets[:], offs)
+        nc.scalar.dma_start(windows[2][:], table_blocks[:, 2, :])
+        nc.sync.dma_start(windows[1][:], table_blocks[:, 1, :])
+        nc.scalar.dma_start(windows[3][:], table_blocks[:, 3, :])
 
         for b in range(blocks):
             pos_wide = held.tile([P, piece], F32, name=f"pos_wide{b}")

@@ -39,7 +39,7 @@ def tile_inpembed_kernel(tc, table, pos, offs, out):
 
             widths = [piece] * pieces
             if b == blocks - 1:
-                widths[-1:] = [piece // 2, piece // 4, piece // 4]
+                widths = [3 * piece // 4, piece // 2, piece // 2, piece // 4]
 
             embedded = held.tile([P, tokens], F32, name=f"embedded{b}")
             first = 0

@@ -50,7 +50,7 @@ def tile_inpembed_kernel(tc, table, pos, offs, out):
                     pos_wide[:, :width],
                     ADD,
                 )
-                queue = nc.sync if k % 2 == 0 else nc.scalar
+                queue = nc.scalar if k % 2 == 0 else nc.sync
                 queue.dma_start(
                     out_blocks[:, b, first : first + width],
                     embedded[:, first : first + width],

import concourse.mybir as mybir

F32, U16 = mybir.dt.float32, mybir.dt.uint16
ADD = mybir.AluOpType.add
COPY = mybir.ActivationFunctionType.Copy
P = 128


def tile_inpembed_kernel(tc, table, pos, offs, out):
    nc = tc.nc
    features, words = table.shape
    tokens = out.shape[1]
    blocks = features // P
    piece = words
    pieces = tokens // piece

    table_blocks = table.rearrange("(p b) s -> p b s", b=blocks)
    pos_blocks = pos.rearrange("(p b) o -> p (b o)", b=blocks)
    out_blocks = out.rearrange("(p b) n -> p b n", b=blocks)

    with tc.tile_pool(name="held", bufs=1) as held:
        pos_cols = held.tile([P, blocks], F32, name="pos_cols")
        offsets = held.tile([P, tokens // 16], U16, name="offsets")
        windows = [held.tile([P, words], F32, name=f"window{b}") for b in range(blocks)]
        nc.sync.dma_start(pos_cols[:], pos_blocks)
        nc.scalar.dma_start(windows[0][:], table_blocks[:, 0, :])
        nc.sync.dma_start(offsets[:], offs)
        nc.scalar.dma_start(windows[2][:], table_blocks[:, 2, :])
        nc.sync.dma_start(windows[1][:], table_blocks[:, 1, :])
        nc.scalar.dma_start(windows[3][:], table_blocks[:, 3, :])

        for b in range(blocks):
            pos_wide = held.tile([P, piece], F32, name=f"pos_wide{b}")
            pos_repeated = pos_cols[:, b : b + 1].to_broadcast([P, piece])
            if b == 0:
                nc.vector.tensor_copy(pos_wide[:], pos_repeated)
            else:
                nc.scalar.activation(pos_wide[:], pos_repeated, COPY)

            widths = [piece] * pieces
            if b == blocks - 1:
                widths = [3 * piece // 4, piece // 2, piece // 2, piece // 4]

            embedded = held.tile([P, tokens], F32, name=f"embedded{b}")
            first = 0
            for k, width in enumerate(widths):
                nc.vector.tensor_tensor(
                    embedded[:, first : first + width],
                    windows[b][:].indirect(offsets[:, first // 16 : (first + width) // 16]),
                    pos_wide[:, :width],
                    ADD,
                )
                queue = nc.scalar if k % 2 == 0 else nc.sync
                queue.dma_start(
                    out_blocks[:, b, first : first + width],
                    embedded[:, first : first + width],
                )
                first += width
